import numpy as np
import ml_dtypes


def mxq(x, axis, fmt="e4m3"):
    dtype, down = {"e4m3": (ml_dtypes.float8_e4m3fn, 7), "e5m2": (ml_dtypes.float8_e5m2, 14)}[fmt]
    v = np.moveaxis(np.asarray(x, np.float32).astype(ml_dtypes.bfloat16).astype(np.float64), axis, -1)
    blocks = v.reshape(v.shape[:-1] + (-1, 32))
    amax = np.abs(blocks).max(-1, keepdims=True)
    byte = np.maximum(np.where(amax > 0, np.frexp(amax)[1] - 1 + 127, 0) - down, 1)
    scale = np.exp2(byte - 127.0)
    codes = (blocks / scale).astype(np.float32).astype(dtype).astype(np.float64)
    return np.moveaxis((codes * scale).reshape(v.shape), -1, axis)


WIDE = False


def mx_kscale(k):
    if not WIDE:
        return np.ones(k)
    levels = np.array([30, -30])
    if k % 512:
        return np.exp2(np.random.permutation(np.resize(levels, k // 32))).repeat(32)
    a = np.empty((k // 512, 16))
    for p in range(k // 512):
        a[p, :8] = np.random.permutation(np.resize(levels, 8))
        for g in range(8):
            far = levels[np.abs(levels - a[p, g]) >= 10]
            a[p, g + 8] = far[np.random.randint(len(far))]
    return np.exp2(a.ravel()).repeat(32)


BF16 = ml_dtypes.bfloat16


def bf(x):
    return np.asarray(x, np.float32).astype(BF16)


def f64(x):
    return np.asarray(x).astype(np.float64)


E2M1 = np.array([0.0, 0.5, 1.0, 1.5, 2.0, 3.0, 4.0, 6.0, -0.0, -0.5, -1.0, -1.5, -2.0, -3.0, -4.0, -6.0])


def pack_weight(w, fmt):
    k, n = w.shape
    w = f64(bf(w)).reshape(k // 32, 32, n)
    amax = np.abs(w).max(1)
    if fmt == "e4m3":
        byte = np.frexp(amax)[1] - 1 + 127 - 7
    else:
        mant, ex = np.frexp(amax / 6.0)
        byte = np.where(mant > 0.5, ex, ex - 1) + 127
    byte = np.clip(np.where(amax > 0, byte, 1), 1, 254)
    scaled = (w * np.exp2(127.0 - byte)[:, None, :]).reshape(k, n).astype(np.float32)
    by_word = np.ascontiguousarray(scaled.reshape(k // 512, 128, 4, n).transpose(0, 1, 3, 2))
    if fmt == "e4m3":
        words = by_word.astype(ml_dtypes.float8_e4m3fn).view(np.uint8)
    else:
        c = by_word.astype(ml_dtypes.float4_e2m1fn).view(np.uint8) & 0xF
        words = c[..., 0::2] | (c[..., 1::2] << 4)
    return np.ascontiguousarray(words), np.ascontiguousarray(byte.astype(np.uint8).reshape(k // 512, 16, n))


def unpack_weight(words, scales, fmt):
    g, p, n, _ = words.shape
    if fmt == "e4m3":
        vals = np.ascontiguousarray(words).view(ml_dtypes.float8_e4m3fn).astype(np.float64)
    else:
        nib = np.empty((g, p, n, 4), np.uint8)
        nib[..., 0::2] = words & 0xF
        nib[..., 1::2] = words >> 4
        vals = E2M1[nib]
    vals = vals * np.repeat(np.exp2(scales.astype(np.float64) - 127.0), 8, axis=1)[..., None]
    return vals.transpose(0, 1, 3, 2).reshape(g * 512, n)

def pack4(w):
    words, scales = pack_weight(w, "e2m1")
    return words.reshape(words.shape[0], 128, -1), scales


def unpack4(words, scales):
    return unpack_weight(words.reshape(words.shape[0], 128, -1, 2), scales, "e2m1")


B, T, NE, NH, NQG, HS = 1, 512, 2048, 16, 4, 128
QPK = NH // NQG
HH = HS // 2


def rope(u, cos, sin):
    u1, u2 = u[..., :HH], u[..., HH:]
    c = cos[None, :, None, :]
    s = sin[None, :, None, :]
    return np.concatenate([u1 * c - u2 * s, u1 * s + u2 * c], axis=-1)


def setup_inputs():
    s = mx_kscale(NE)
    inv_freq = 1.0 / 10000.0 ** (np.arange(HH) / HH)
    ang = np.outer(np.arange(T), inv_freq)
    x = bf(np.random.standard_normal((B, T, NE)) * s)
    w = np.random.standard_normal(((NH + 2 * NQG) * HS, NE)) / np.sqrt(NE) / s[None, :]
    words, scales = pack4(np.ascontiguousarray(w.T))
    return {"x": x,
            "cos": bf(np.cos(ang)), "sin": bf(np.sin(ang)),
            "W_attn_words": words, "W_attn_scales": scales}


def reference(x, cos, sin, W_attn_words, W_attn_scales):
    qkv = mxq(f64(x), 2, "e5m2") @ unpack4(W_attn_words, W_attn_scales)
    qkv = qkv.reshape(B, T, NQG, QPK + 2, HS)
    q = qkv[..., :QPK, :].reshape(B, T, NH, HS)
    k = qkv[..., QPK, :]
    v = qkv[..., QPK + 1, :]
    return rope(q, f64(cos), f64(sin)), rope(k, f64(cos), f64(sin)), v

@@ -1,0 +1,216 @@
+from contextlib import ExitStack
+
+import concourse.mybir as mybir
+from concourse.masks import make_identity
+
+F32 = mybir.dt.float32
+BF16 = mybir.dt.bfloat16
+I32 = mybir.dt.int32
+U32 = mybir.dt.uint32
+U8 = mybir.dt.uint8
+E5M2X4 = mybir.dt.float8_e5m2_x4
+E2M1X4 = mybir.dt.float4_e2m1fn_x4
+ADD = mybir.AluOpType.add
+MULT = mybir.AluOpType.mult
+
+T, NE, NOUT = 512, 2048, 3072
+FLOPS = 2 * T * NE * NOUT
+
+P = 128
+PASSES = NE // 512
+MT = T // P
+GROUPS = 4
+GCOLS = 768
+HS = 128
+HH = 64
+
+
+def tile_causalselfattention_pa_kernel(tc, x, cos, sin, w_words, w_scales, out_q, out_k, out_v):
+    nc = tc.nc
+    with ExitStack() as ctx:
+        keep = ctx.enter_context(tc.tile_pool(name="keep", bufs=1))
+        prod_pool = ctx.enter_context(tc.tile_pool(name="prod", bufs=3))
+        res_pool = ctx.enter_context(tc.tile_pool(name="res", bufs=3))
+        vres_pool = ctx.enter_context(tc.tile_pool(name="vres", bufs=4))
+        psum = ctx.enter_context(tc.psum_pool(name="psum", bufs=8))
+
+        ident = keep.tile([P, P], F32, name="ident")
+        make_identity(nc, ident[:])
+
+        xs = [keep.tile([P, NE], BF16, name="xs%d" % m, align_bytes=64) for m in range(MT)]
+        xg = [keep.tile([P, NE], BF16, name="xg%d" % m, align_bytes=64) for m in range(MT)]
+        xc = [keep.tile([P, NE // 4], U32, name="xc%d" % m, align_bytes=64) for m in range(MT)]
+        xsc = [keep.tile([P, NE // 4], U8, name="xsc%d" % m, align_bytes=64) for m in range(MT)]
+        wq = [keep.tile([P, PASSES, 1024], U8, name="wq%d" % g, align_bytes=64) for g in range(GROUPS)]
+        wk = keep.tile([P, PASSES, 1024], U8, name="wk", align_bytes=64)
+        wv = keep.tile([P, PASSES, 1024], U8, name="wv", align_bytes=64)
+        sc_all = keep.tile([P, GROUPS, PASSES, GCOLS], U8, name="sc_all", align_bytes=64)
+        sck = keep.tile([P, PASSES, 512], U8, name="sck", align_bytes=64)
+        scv = keep.tile([P, PASSES, 512], U8, name="scv", align_bytes=64)
+        craw = keep.tile([P, MT, HH], BF16, name="craw")
+        sraw = keep.tile([P, MT, HH], BF16, name="sraw")
+        tab = keep.tile([P, MT, 2, HS], F32, name="tab")
+        warm_in = keep.tile([P, 8], F32, name="warm_in")
+        warm_out = keep.tile([P, 8], F32, name="warm_out")
+
+        with tc.manual_schedule():
+            nc.vector.memset(warm_in[:], 0.0)
+            nc.scalar.copy(out=warm_out[:], in_=warm_in[:])
+            for grp in range(GROUPS):
+                nc.vector.memset(sc_all[:, grp].rearrange("p g n -> p (g n)").bitcast(I32), 0)
+
+            def load_x(m):
+                nc.sync.dma_start(out=xs[m][:], in_=x[0, P * m : P * (m + 1), :])
+
+            def load_scales(grp):
+                for qd in range(4):
+                    nc.sync.dma_start(
+                        out=sc_all[32 * qd : 32 * qd + 4, grp, :, :].bitcast(I32),
+                        in_=w_scales[:, 4 * qd : 4 * qd + 4, GCOLS * grp : GCOLS * (grp + 1)]
+                        .rearrange("g r n -> r g n")
+                        .bitcast(I32),
+                    )
+
+            def load_wq(grp):
+                nc.sync.dma_start(
+                    out=wq[grp][:].bitcast(I32),
+                    in_=w_words[:, :, 2 * GCOLS * grp : 2 * GCOLS * grp + 1024].rearrange("g p b -> p g b").bitcast(I32),
+                )
+
+            def load_wkv(dst, first_byte):
+                for g in range(PASSES):
+                    nc.sync.dma_start(
+                        out=dst[:, g, :].bitcast(I32).rearrange("p (grp c) -> p grp c", grp=GROUPS),
+                        in_=w_words[g].rearrange("p (grp c) -> p grp c", grp=GROUPS)[:, :, first_byte : first_byte + 256].bitcast(I32),
+                    )
+
+            load_x(0)
+            load_x(1)
+            load_scales(0)
+            load_wq(0)
+            nc.sync.dma_start(out=craw[:], in_=cos.rearrange("(m p) i -> p m i", p=P))
+            nc.sync.dma_start(out=sraw[:], in_=sin.rearrange("(m p) i -> p m i", p=P))
+            load_x(2)
+            load_x(3)
+            load_scales(1)
+            load_wq(1)
+            load_scales(2)
+            load_wq(2)
+            load_scales(3)
+            load_wkv(wv, 1280)
+            load_wq(3)
+            load_wkv(wk, 1024)
+
+            nc.gpsimd.tensor_scalar(
+                out=tab[:, :, 0, :].rearrange("p m (s i) -> p m s i", s=2),
+                in0=craw[:].unsqueeze(2).to_broadcast([P, MT, 2, HH]),
+                scalar1=1.0, scalar2=0.0, op0=MULT, op1=ADD,
+            )
+            nc.gpsimd.tensor_scalar(out=tab[:, :, 1, 0:HH], in0=sraw[:], scalar1=1.0, scalar2=0.0, op0=MULT, op1=ADD)
+            nc.gpsimd.tensor_scalar(out=tab[:, :, 1, HH:HS], in0=sraw[:], scalar1=-1.0, scalar2=0.0, op0=MULT, op1=ADD)
+
+            def transpose_x(m, both_engines):
+                words = xs[m][:].bitcast(F32)
+                grouped = xg[m][:].bitcast(F32).rearrange("p (g r u) -> p g r u", g=PASSES, u=2)
+                for b in range(2):
+                    xt = psum.tile([P, 512], F32, name="bank", tag="bank")
+                    for gl in range(2):
+                        g = 2 * b + gl
+                        for u in range(2):
+                            nc.tensor.transpose(
+                                out=xt[:, P * (2 * gl + u) : P * (2 * gl + u + 1)],
+                                in_=words[:, 256 * g + u : 256 * (g + 1) : 2],
+                                identity=ident[:],
+                            )
+                    src = xt[:].rearrange("p (gl u r) -> p gl r u", gl=2, u=2)
+                    if both_engines and b == 0:
+                        nc.vector.tensor_copy(out=grouped[:, 2 * b : 2 * b + 2], in_=src)
+                    else:
+                        nc.scalar.copy(out=grouped[:, 2 * b : 2 * b + 2], in_=src)
+
+            def quantize_x(m):
+                nc.vector.quantize_mx(out=xc[m][:].bitcast(E5M2X4), scales=xsc[m][:], in_=xg[m][:])
+
+            def project(m, codes, scales):
+                acc = psum.tile([P, 512], F32, name="bank", tag="bank")
+                for g in range(PASSES):
+                    nc.tensor.matmul_mx(
+                        out=acc[:],
+                        lhsT=xc[m][:, P * g : P * (g + 1)].bitcast(E5M2X4),
+                        lhsT_scale=xsc[m][:, P * g : P * (g + 1)],
+                        rhs=codes[:, g, :].bitcast(E2M1X4),
+                        rhs_scale=scales[:, g, 0:512],
+                        start=(g == 0),
+                        stop=(g == PASSES - 1),
+                    )
+                return acc
+
+            def products(m, acc, dst):
+                nc.vector.tensor_tensor(
+                    out=dst.rearrange("p w (h e) -> p w h e", h=4),
+                    in0=acc[:].rearrange("p (h e) -> p h e", h=4).unsqueeze(1).to_broadcast([P, 2, 4, HS]),
+                    in1=tab[:, m].unsqueeze(2).to_broadcast([P, 2, 4, HS]),
+                    op=MULT,
+                )
+
+            def combine(engine, prod, res):
+                engine.tensor_tensor(
+                    out=res.rearrange("p (h s i) -> p h s i", s=2, i=HH),
+                    in0=prod[:, 0].rearrange("p (h s i) -> p h s i", s=2, i=HH),
+                    in1=prod[:, 1].rearrange("p (h s i) -> p h s i", s=2, i=HH)[:, :, ::-1, :],
+                    op=ADD,
+                )
+
+            def rotated(m0, n, codes, scales, dst, sum_engine):
+                prod = prod_pool.tile([P, 2, n * 512], F32, name="prod%d" % n)
+                for tl in range(n):
+                    acc = project(m0 + tl, codes, scales)
+                    products(m0 + tl, acc, prod[:, :, 512 * tl : 512 * (tl + 1)])
+                res = res_pool.tile([P, n * 512], F32, name="res%d" % n)
+                combine(sum_engine, prod, res[:])
+                nc.sync.dma_start(
+                    out=dst.rearrange("(tl p) h e -> p tl (h e)", p=P),
+                    in_=res[:].rearrange("p (tl c) -> p tl c", tl=n),
+                )
+
+            def q_pair(m0, grp):
+                rotated(m0, 2, wq[grp], sc_all[:, grp], out_q[0, P * m0 : P * (m0 + 2), 4 * grp : 4 * grp + 4, :], nc.gpsimd)
+
+            def v_tile(m):
+                acc = project(m, wv, scv)
+                res = vres_pool.tile([P, 512], F32, name="vres")
+                nc.scalar.copy(out=res[:], in_=acc[:])
+                nc.scalar.dma_start(out=out_v[0, P * m : P * (m + 1), :, :], in_=res[:].rearrange("p (h e) -> p h e", h=4))
+
+            transpose_x(0, True)
+            transpose_x(1, True)
+            quantize_x(0)
+            quantize_x(1)
+            q_pair(0, 0)
+            transpose_x(2, False)
+            transpose_x(3, False)
+            quantize_x(2)
+            quantize_x(3)
+            q_pair(0, 1)
+            q_pair(2, 0)
+            nat = sc_all[:].bitcast(I32)
+            nc.vector.tensor_copy(
+                out=scv[:].bitcast(I32).rearrange("p g (grp c) -> p g grp c", grp=GROUPS),
+                in_=nat[:, :, :, 160:192].rearrange("p grp g c -> p g grp c"),
+            )
+            q_pair(2, 1)
+            v_tile(0)
+            q_pair(0, 2)
+            nc.vector.tensor_copy(
+                out=sck[:].bitcast(I32).rearrange("p g (grp c) -> p g grp c", grp=GROUPS),
+                in_=nat[:, :, :, 128:160].rearrange("p grp g c -> p g grp c"),
+            )
+            q_pair(2, 2)
+            v_tile(1)
+            q_pair(0, 3)
+            q_pair(2, 3)
+            rotated(0, 2, wk, sck, out_k[0, 0 : 2 * P, :, :], nc.gpsimd)
+            rotated(2, 1, wk, sck, out_k[0, 2 * P : 3 * P, :, :], nc.gpsimd)
+            rotated(3, 1, wk, sck, out_k[0, 3 * P : 4 * P, :, :], nc.vector)
+            v_tile(2)
+            v_tile(3)

@@ -38,6 +38,7 @@ def tile_causalselfattention_pa_kernel(tc, x, cos, sin, w_words, w_scales, out_q
         make_identity(nc, ident[:])
 
         xs = [keep.tile([P, NE], BF16, name="xs%d" % m, align_bytes=64) for m in range(MT)]
+        xo = [keep.tile([P, NE // 2], F32, name="xo%d" % m, align_bytes=64) for m in range(MT)]
         xg = [keep.tile([P, NE], BF16, name="xg%d" % m, align_bytes=64) for m in range(MT)]
         xc = [keep.tile([P, NE // 4], U32, name="xc%d" % m, align_bytes=64) for m in range(MT)]
         xsc = [keep.tile([P, NE // 4], U8, name="xsc%d" % m, align_bytes=64) for m in range(MT)]
@@ -52,15 +53,22 @@ def tile_causalselfattention_pa_kernel(tc, x, cos, sin, w_words, w_scales, out_q
         tab = keep.tile([P, MT, 2, HS], F32, name="tab")
         warm_in = keep.tile([P, 8], F32, name="warm_in")
         warm_out = keep.tile([P, 8], F32, name="warm_out")
+        zeros = keep.tile([P, 512], BF16, name="zeros")
+
+        x_t = x[0].rearrange("(p m) k -> m p k", m=MT)
+        q_t = out_q[0].rearrange("(p m) h e -> p m (h e)", m=MT)
+        k_t = out_k[0].rearrange("(p m) h e -> p m (h e)", m=MT)
+        v_t = out_v[0].rearrange("(p m) h e -> p m (h e)", m=MT)
 
         with tc.manual_schedule():
+            nc.gpsimd.memset(zeros[:], 0.0)
             nc.vector.memset(warm_in[:], 0.0)
             nc.scalar.copy(out=warm_out[:], in_=warm_in[:])
             for grp in range(GROUPS):
                 nc.vector.memset(sc_all[:, grp].rearrange("p g n -> p (g n)").bitcast(I32), 0)
 
             def load_x(m):
-                nc.sync.dma_start(out=xs[m][:], in_=x[0, P * m : P * (m + 1), :])
+                nc.sync.dma_start(out=xs[m][:], in_=x_t[m])
 
             def load_scales(grp):
                 for qd in range(4):
@@ -88,40 +96,44 @@ def tile_causalselfattention_pa_kernel(tc, x, cos, sin, w_words, w_scales, out_q
             load_x(1)
             load_scales(0)
             load_wq(0)
-            nc.sync.dma_start(out=craw[:], in_=cos.rearrange("(m p) i -> p m i", p=P))
-            nc.sync.dma_start(out=sraw[:], in_=sin.rearrange("(m p) i -> p m i", p=P))
+            nc.sync.dma_start(out=craw[:], in_=cos.rearrange("(p m) i -> p m i", m=MT))
+            nc.sync.dma_start(out=sraw[:], in_=sin.rearrange("(p m) i -> p m i", m=MT))
             load_x(2)
-            load_x(3)
             load_scales(1)
             load_wq(1)
+            load_x(3)
             load_scales(2)
             load_wq(2)
             load_scales(3)
-            load_wkv(wv, 1280)
             load_wq(3)
+            load_wkv(wv, 1280)
             load_wkv(wk, 1024)
 
-            nc.gpsimd.tensor_scalar(
-                out=tab[:, :, 0, :].rearrange("p m (s i) -> p m s i", s=2),
-                in0=craw[:].unsqueeze(2).to_broadcast([P, MT, 2, HH]),
-                scalar1=1.0, scalar2=0.0, op0=MULT, op1=ADD,
-            )
-            nc.gpsimd.tensor_scalar(out=tab[:, :, 1, 0:HH], in0=sraw[:], scalar1=1.0, scalar2=0.0, op0=MULT, op1=ADD)
-            nc.gpsimd.tensor_scalar(out=tab[:, :, 1, HH:HS], in0=sraw[:], scalar1=-1.0, scalar2=0.0, op0=MULT, op1=ADD)
+            idle_bank = psum.tile([P, 512], F32, name="bank", tag="bank")
 
-            def transpose_x(m, both_engines):
+            def keep_warm(n):
+                for i in range(n):
+                    nc.tensor.matmul(out=idle_bank[:], lhsT=zeros[:, 0:P], rhs=zeros[:], start=True, stop=True)
+
+            def transpose_x(m, reorder_first, both_engines):
                 words = xs[m][:].bitcast(F32)
                 grouped = xg[m][:].bitcast(F32).rearrange("p (g r u) -> p g r u", g=PASSES, u=2)
+                if reorder_first:
+                    for b in range(2):
+                        nc.scalar.copy(
+                            out=xo[m][:, 512 * b : 512 * (b + 1)].rearrange("p (gl u r) -> p gl u r", gl=2, u=2),
+                            in_=words[:, 512 * b : 512 * (b + 1)].rearrange("p (gl r u) -> p gl u r", gl=2, u=2),
+                        )
                 for b in range(2):
                     xt = psum.tile([P, 512], F32, name="bank", tag="bank")
                     for gl in range(2):
                         g = 2 * b + gl
                         for u in range(2):
-                            nc.tensor.transpose(
-                                out=xt[:, P * (2 * gl + u) : P * (2 * gl + u + 1)],
-                                in_=words[:, 256 * g + u : 256 * (g + 1) : 2],
-                                identity=ident[:],
-                            )
+                            if reorder_first:
+                                src_words = xo[m][:, P * (2 * g + u) : P * (2 * g + u + 1)]
+                            else:
+                                src_words = words[:, 256 * g + u : 256 * (g + 1) : 2]
+                            nc.tensor.transpose(out=xt[:, P * (2 * gl + u) : P * (2 * gl + u + 1)], in_=src_words, identity=ident[:])
                     src = xt[:].rearrange("p (gl u r) -> p gl r u", gl=2, u=2)
                     if both_engines and b == 0:
                         nc.vector.tensor_copy(out=grouped[:, 2 * b : 2 * b + 2], in_=src)
@@ -145,72 +157,85 @@ def tile_causalselfattention_pa_kernel(tc, x, cos, sin, w_words, w_scales, out_q
                     )
                 return acc
 
-            def products(m, acc, dst):
-                nc.vector.tensor_tensor(
-                    out=dst.rearrange("p w (h e) -> p w h e", h=4),
-                    in0=acc[:].rearrange("p (h e) -> p h e", h=4).unsqueeze(1).to_broadcast([P, 2, 4, HS]),
-                    in1=tab[:, m].unsqueeze(2).to_broadcast([P, 2, 4, HS]),
-                    op=MULT,
-                )
-
-            def combine(engine, prod, res):
-                engine.tensor_tensor(
-                    out=res.rearrange("p (h s i) -> p h s i", s=2, i=HH),
+            def rotated(tiles, dst, sum_engine):
+                n = len(tiles)
+                prod = prod_pool.tile([P, 2, n * 512], F32, name="prod%d" % n)
+                for tl in range(n):
+                    m, codes, scales = tiles[tl]
+                    acc = project(m, codes, scales)
+                    nc.vector.tensor_tensor(
+                        out=prod[:, :, 512 * tl : 512 * (tl + 1)].rearrange("p w (h e) -> p w h e", h=4),
+                        in0=acc[:].rearrange("p (h e) -> p h e", h=4).unsqueeze(1).to_broadcast([P, 2, 4, HS]),
+                        in1=tab[:, m].unsqueeze(2).to_broadcast([P, 2, 4, HS]),
+                        op=MULT,
+                    )
+                res = res_pool.tile([P, n * 512], F32, name="res%d" % n)
+                sum_engine.tensor_tensor(
+                    out=res[:].rearrange("p (h s i) -> p h s i", s=2, i=HH),
                     in0=prod[:, 0].rearrange("p (h s i) -> p h s i", s=2, i=HH),
                     in1=prod[:, 1].rearrange("p (h s i) -> p h s i", s=2, i=HH)[:, :, ::-1, :],
                     op=ADD,
                 )
+                nc.sync.dma_start(out=dst, in_=res[:].rearrange("p (tl c) -> p tl c", tl=n))
 
-            def rotated(m0, n, codes, scales, dst, sum_engine):
-                prod = prod_pool.tile([P, 2, n * 512], F32, name="prod%d" % n)
-                for tl in range(n):
-                    acc = project(m0 + tl, codes, scales)
-                    products(m0 + tl, acc, prod[:, :, 512 * tl : 512 * (tl + 1)])
-                res = res_pool.tile([P, n * 512], F32, name="res%d" % n)
-                combine(sum_engine, prod, res[:])
-                nc.sync.dma_start(
-                    out=dst.rearrange("(tl p) h e -> p tl (h e)", p=P),
-                    in_=res[:].rearrange("p (tl c) -> p tl c", tl=n),
+            def q_two_tokens(m0, grp):
+                rotated(
+                    [(m0 + tl, wq[grp], sc_all[:, grp]) for tl in range(2)],
+                    q_t[:, m0 : m0 + 2, 512 * grp : 512 * (grp + 1)],
+                    nc.gpsimd,
                 )
 
-            def q_pair(m0, grp):
-                rotated(m0, 2, wq[grp], sc_all[:, grp], out_q[0, P * m0 : P * (m0 + 2), 4 * grp : 4 * grp + 4, :], nc.gpsimd)
+            def q_two_groups(m, grp0):
+                rotated(
+                    [(m, wq[grp0 + tl], sc_all[:, grp0 + tl]) for tl in range(2)],
+                    q_t[:, m, 512 * grp0 : 512 * (grp0 + 2)].rearrange("p (tl c) -> p tl c", tl=2),
+                    nc.gpsimd,
+                )
 
             def v_tile(m):
                 acc = project(m, wv, scv)
                 res = vres_pool.tile([P, 512], F32, name="vres")
                 nc.scalar.copy(out=res[:], in_=acc[:])
-                nc.scalar.dma_start(out=out_v[0, P * m : P * (m + 1), :, :], in_=res[:].rearrange("p (h e) -> p h e", h=4))
+                nc.scalar.dma_start(out=v_t[:, m, :], in_=res[:])
 
-            transpose_x(0, True)
-            transpose_x(1, True)
+            keep_warm(5)
+            transpose_x(0, False, True)
             quantize_x(0)
+            keep_warm(1)
+            transpose_x(1, False, True)
             quantize_x(1)
-            q_pair(0, 0)
-            transpose_x(2, False)
-            transpose_x(3, False)
+            keep_warm(2)
+            nc.vector.tensor_copy(
+                out=tab[:, :, 0, :].rearrange("p m (s i) -> p m s i", s=2),
+                in_=craw[:].unsqueeze(2).to_broadcast([P, MT, 2, HH]),
+            )
+            nc.scalar.copy(out=tab[:, :, 1, 0:HH], in_=sraw[:])
+            nc.scalar.mul(out=tab[:, :, 1, HH:HS], in_=sraw[:], mul=-1.0)
+            q_two_tokens(0, 0)
+            transpose_x(2, True, False)
             quantize_x(2)
+            q_two_tokens(0, 1)
+            transpose_x(3, True, False)
             quantize_x(3)
-            q_pair(0, 1)
-            q_pair(2, 0)
+            q_two_groups(2, 0)
+            q_two_groups(3, 0)
             nat = sc_all[:].bitcast(I32)
             nc.vector.tensor_copy(
                 out=scv[:].bitcast(I32).rearrange("p g (grp c) -> p g grp c", grp=GROUPS),
                 in_=nat[:, :, :, 160:192].rearrange("p grp g c -> p g grp c"),
             )
-            q_pair(2, 1)
+            q_two_groups(0, 2)
+            q_two_groups(1, 2)
             v_tile(0)
-            q_pair(0, 2)
             nc.vector.tensor_copy(
                 out=sck[:].bitcast(I32).rearrange("p g (grp c) -> p g grp c", grp=GROUPS),
                 in_=nat[:, :, :, 128:160].rearrange("p grp g c -> p g grp c"),
             )
-            q_pair(2, 2)
+            q_two_groups(2, 2)
+            q_two_groups(3, 2)
             v_tile(1)
-            q_pair(0, 3)
-            q_pair(2, 3)
-            rotated(0, 2, wk, sck, out_k[0, 0 : 2 * P, :, :], nc.gpsimd)
-            rotated(2, 1, wk, sck, out_k[0, 2 * P : 3 * P, :, :], nc.gpsimd)
-            rotated(3, 1, wk, sck, out_k[0, 3 * P : 4 * P, :, :], nc.vector)
+            rotated([(0, wk, sck), (1, wk, sck)], k_t[:, 0:2, :], nc.gpsimd)
+            rotated([(2, wk, sck)], k_t[:, 2:3, :], nc.gpsimd)
+            rotated([(3, wk, sck)], k_t[:, 3:4, :], nc.vector)
             v_tile(2)
             v_tile(3)

@@ -29,8 +29,8 @@ def tile_causalselfattention_pa_kernel(tc, x, cos, sin, w_words, w_scales, out_q
     nc = tc.nc
     with ExitStack() as ctx:
         keep = ctx.enter_context(tc.tile_pool(name="keep", bufs=1))
-        prod_pool = ctx.enter_context(tc.tile_pool(name="prod", bufs=3))
-        res_pool = ctx.enter_context(tc.tile_pool(name="res", bufs=3))
+        prod_pool = ctx.enter_context(tc.tile_pool(name="prod", bufs=4))
+        res_pool = ctx.enter_context(tc.tile_pool(name="res", bufs=4))
         vres_pool = ctx.enter_context(tc.tile_pool(name="vres", bufs=4))
         psum = ctx.enter_context(tc.psum_pool(name="psum", bufs=8))
 
@@ -38,11 +38,11 @@ def tile_causalselfattention_pa_kernel(tc, x, cos, sin, w_words, w_scales, out_q
         make_identity(nc, ident[:])
 
         xs = [keep.tile([P, NE], BF16, name="xs%d" % m, align_bytes=64) for m in range(MT)]
-        xo = [keep.tile([P, NE // 2], F32, name="xo%d" % m, align_bytes=64) for m in range(MT)]
-        xg = [keep.tile([P, NE], BF16, name="xg%d" % m, align_bytes=64) for m in range(MT)]
-        xc = [keep.tile([P, NE // 4], U32, name="xc%d" % m, align_bytes=64) for m in range(MT)]
-        xsc = [keep.tile([P, NE // 4], U8, name="xsc%d" % m, align_bytes=64) for m in range(MT)]
-        wq = [keep.tile([P, PASSES, 1024], U8, name="wq%d" % g, align_bytes=64) for g in range(GROUPS)]
+        xg = [[keep.tile([P, NE // 2], BF16, name="xg%d_%d" % (m, b), align_bytes=64) for b in range(2)] for m in range(MT)]
+        xc = [[keep.tile([P, NE // 8], U32, name="xc%d_%d" % (m, b), align_bytes=64) for b in range(2)] for m in range(MT)]
+        xsc = [[keep.tile([P, NE // 8], U8, name="xsc%d_%d" % (m, b), align_bytes=64) for b in range(2)] for m in range(MT)]
+        wq0 = [keep.tile([P, 1024], U8, name="wq0g%d" % g, align_bytes=64) for g in range(PASSES)]
+        wq = [None] + [keep.tile([P, PASSES, 1024], U8, name="wq%d" % grp, align_bytes=64) for grp in range(1, GROUPS)]
         wk = keep.tile([P, PASSES, 1024], U8, name="wk", align_bytes=64)
         wv = keep.tile([P, PASSES, 1024], U8, name="wv", align_bytes=64)
         sc_all = keep.tile([P, GROUPS, PASSES, GCOLS], U8, name="sc_all", align_bytes=64)
@@ -60,8 +60,16 @@ def tile_causalselfattention_pa_kernel(tc, x, cos, sin, w_words, w_scales, out_q
         k_t = out_k[0].rearrange("(p m) h e -> p m (h e)", m=MT)
         v_t = out_v[0].rearrange("(p m) h e -> p m (h e)", m=MT)
 
+        def passes_of(codes, scales):
+            return [(codes[:, g, :], scales[:, g, 0:512]) for g in range(PASSES)]
+
+        w_q = [[(wq0[g][:], sc_all[:, 0, g, 0:512]) for g in range(PASSES)]]
+        w_q += [passes_of(wq[grp], sc_all[:, grp]) for grp in range(1, GROUPS)]
+        w_k = passes_of(wk, sck)
+        w_v = passes_of(wv, scv)
+
         with tc.manual_schedule():
-            nc.gpsimd.memset(zeros[:], 0.0)
+            nc.vector.memset(zeros[:], 0.0)
             nc.vector.memset(warm_in[:], 0.0)
             nc.scalar.copy(out=warm_out[:], in_=warm_in[:])
             for grp in range(GROUPS):
@@ -95,19 +103,15 @@ def tile_causalselfattention_pa_kernel(tc, x, cos, sin, w_words, w_scales, out_q
             load_x(0)
             load_x(1)
             load_scales(0)
-            load_wq(0)
+            for g in range(PASSES):
+                nc.sync.dma_start(out=wq0[g][:].bitcast(I32), in_=w_words[g, :, 0:1024].bitcast(I32))
             nc.sync.dma_start(out=craw[:], in_=cos.rearrange("(p m) i -> p m i", m=MT))
             nc.sync.dma_start(out=sraw[:], in_=sin.rearrange("(p m) i -> p m i", m=MT))
             load_x(2)
-            load_scales(1)
-            load_wq(1)
             load_x(3)
-            load_scales(2)
-            load_wq(2)
-            load_scales(3)
-            load_wq(3)
-            load_wkv(wv, 1280)
-            load_wkv(wk, 1024)
+            for grp in range(1, GROUPS):
+                load_scales(grp)
+                load_wq(grp)
 
             idle_bank = psum.tile([P, 512], F32, name="bank", tag="bank")
 
@@ -115,43 +119,39 @@ def tile_causalselfattention_pa_kernel(tc, x, cos, sin, w_words, w_scales, out_q
                 for i in range(n):
                     nc.tensor.matmul(out=idle_bank[:], lhsT=zeros[:, 0:P], rhs=zeros[:], start=True, stop=True)
 
-            def transpose_x(m, reorder_first, both_engines):
+            def transpose_x(m, both_engines):
                 words = xs[m][:].bitcast(F32)
-                grouped = xg[m][:].bitcast(F32).rearrange("p (g r u) -> p g r u", g=PASSES, u=2)
-                if reorder_first:
-                    for b in range(2):
-                        nc.scalar.copy(
-                            out=xo[m][:, 512 * b : 512 * (b + 1)].rearrange("p (gl u r) -> p gl u r", gl=2, u=2),
-                            in_=words[:, 512 * b : 512 * (b + 1)].rearrange("p (gl r u) -> p gl u r", gl=2, u=2),
-                        )
                 for b in range(2):
+                    grouped = xg[m][b][:].bitcast(F32).rearrange("p (gl r u) -> p gl r u", gl=2, u=2)
                     xt = psum.tile([P, 512], F32, name="bank", tag="bank")
                     for gl in range(2):
                         g = 2 * b + gl
                         for u in range(2):
-                            if reorder_first:
-                                src_words = xo[m][:, P * (2 * g + u) : P * (2 * g + u + 1)]
-                            else:
-                                src_words = words[:, 256 * g + u : 256 * (g + 1) : 2]
-                            nc.tensor.transpose(out=xt[:, P * (2 * gl + u) : P * (2 * gl + u + 1)], in_=src_words, identity=ident[:])
+                            nc.tensor.transpose(
+                                out=xt[:, P * (2 * gl + u) : P * (2 * gl + u + 1)],
+                                in_=words[:, 256 * g + u : 256 * (g + 1) : 2],
+                                identity=ident[:],
+                            )
                     src = xt[:].rearrange("p (gl u r) -> p gl r u", gl=2, u=2)
                     if both_engines and b == 0:
-                        nc.vector.tensor_copy(out=grouped[:, 2 * b : 2 * b + 2], in_=src)
+                        nc.vector.tensor_copy(out=grouped, in_=src)
                     else:
-                        nc.scalar.copy(out=grouped[:, 2 * b : 2 * b + 2], in_=src)
+                        nc.scalar.copy(out=grouped, in_=src)
 
             def quantize_x(m):
-                nc.vector.quantize_mx(out=xc[m][:].bitcast(E5M2X4), scales=xsc[m][:], in_=xg[m][:])
+                for b in range(2):
+                    nc.vector.quantize_mx(out=xc[m][b][:].bitcast(E5M2X4), scales=xsc[m][b][:], in_=xg[m][b][:])
 
-            def project(m, codes, scales):
+            def project(m, w_tile):
                 acc = psum.tile([P, 512], F32, name="bank", tag="bank")
                 for g in range(PASSES):
+                    codes, scales = w_tile[g]
                     nc.tensor.matmul_mx(
                         out=acc[:],
-                        lhsT=xc[m][:, P * g : P * (g + 1)].bitcast(E5M2X4),
-                        lhsT_scale=xsc[m][:, P * g : P * (g + 1)],
-                        rhs=codes[:, g, :].bitcast(E2M1X4),
-                        rhs_scale=scales[:, g, 0:512],
+                        lhsT=xc[m][g // 2][:, P * (g % 2) : P * (g % 2 + 1)].bitcast(E5M2X4),
+                        lhsT_scale=xsc[m][g // 2][:, P * (g % 2) : P * (g % 2 + 1)],
+                        rhs=codes.bitcast(E2M1X4),
+                        rhs_scale=scales,
                         start=(g == 0),
                         stop=(g == PASSES - 1),
                     )
@@ -161,8 +161,8 @@ def tile_causalselfattention_pa_kernel(tc, x, cos, sin, w_words, w_scales, out_q
                 n = len(tiles)
                 prod = prod_pool.tile([P, 2, n * 512], F32, name="prod%d" % n)
                 for tl in range(n):
-                    m, codes, scales = tiles[tl]
-                    acc = project(m, codes, scales)
+                    m, w_tile = tiles[tl]
+                    acc = project(m, w_tile)
                     nc.vector.tensor_tensor(
                         out=prod[:, :, 512 * tl : 512 * (tl + 1)].rearrange("p w (h e) -> p w h e", h=4),
                         in0=acc[:].rearrange("p (h e) -> p h e", h=4).unsqueeze(1).to_broadcast([P, 2, 4, HS]),
@@ -179,32 +179,27 @@ def tile_causalselfattention_pa_kernel(tc, x, cos, sin, w_words, w_scales, out_q
                 nc.sync.dma_start(out=dst, in_=res[:].rearrange("p (tl c) -> p tl c", tl=n))
 
             def q_two_tokens(m0, grp):
-                rotated(
-                    [(m0 + tl, wq[grp], sc_all[:, grp]) for tl in range(2)],
-                    q_t[:, m0 : m0 + 2, 512 * grp : 512 * (grp + 1)],
-                    nc.gpsimd,
-                )
+                rotated([(m0 + tl, w_q[grp]) for tl in range(2)], q_t[:, m0 : m0 + 2, 512 * grp : 512 * (grp + 1)], nc.gpsimd)
 
             def q_two_groups(m, grp0):
                 rotated(
-                    [(m, wq[grp0 + tl], sc_all[:, grp0 + tl]) for tl in range(2)],
+                    [(m, w_q[grp0 + tl]) for tl in range(2)],
                     q_t[:, m, 512 * grp0 : 512 * (grp0 + 2)].rearrange("p (tl c) -> p tl c", tl=2),
                     nc.gpsimd,
                 )
 
             def v_tile(m):
-                acc = project(m, wv, scv)
+                acc = project(m, w_v)
                 res = vres_pool.tile([P, 512], F32, name="vres")
                 nc.scalar.copy(out=res[:], in_=acc[:])
                 nc.scalar.dma_start(out=v_t[:, m, :], in_=res[:])
 
-            keep_warm(5)
-            transpose_x(0, False, True)
+            keep_warm(4)
+            transpose_x(0, True)
             quantize_x(0)
             keep_warm(1)
-            transpose_x(1, False, True)
+            transpose_x(1, True)
             quantize_x(1)
-            keep_warm(2)
             nc.vector.tensor_copy(
                 out=tab[:, :, 0, :].rearrange("p m (s i) -> p m s i", s=2),
                 in_=craw[:].unsqueeze(2).to_broadcast([P, MT, 2, HH]),
@@ -212,13 +207,15 @@ def tile_causalselfattention_pa_kernel(tc, x, cos, sin, w_words, w_scales, out_q
             nc.scalar.copy(out=tab[:, :, 1, 0:HH], in_=sraw[:])
             nc.scalar.mul(out=tab[:, :, 1, HH:HS], in_=sraw[:], mul=-1.0)
             q_two_tokens(0, 0)
-            transpose_x(2, True, False)
+            load_wkv(wv, 1280)
+            transpose_x(2, False)
             quantize_x(2)
-            q_two_tokens(0, 1)
-            transpose_x(3, True, False)
+            transpose_x(3, False)
             quantize_x(3)
-            q_two_groups(2, 0)
-            q_two_groups(3, 0)
+            q_two_tokens(2, 0)
+            q_two_tokens(0, 1)
+            load_wkv(wk, 1024)
+            q_two_tokens(2, 1)
             nat = sc_all[:].bitcast(I32)
             nc.vector.tensor_copy(
                 out=scv[:].bitcast(I32).rearrange("p g (grp c) -> p g grp c", grp=GROUPS),
@@ -234,8 +231,8 @@ def tile_causalselfattention_pa_kernel(tc, x, cos, sin, w_words, w_scales, out_q
             q_two_groups(2, 2)
             q_two_groups(3, 2)
             v_tile(1)
-            rotated([(0, wk, sck), (1, wk, sck)], k_t[:, 0:2, :], nc.gpsimd)
-            rotated([(2, wk, sck)], k_t[:, 2:3, :], nc.gpsimd)
-            rotated([(3, wk, sck)], k_t[:, 3:4, :], nc.vector)
+            rotated([(0, w_k), (1, w_k)], k_t[:, 0:2, :], nc.gpsimd)
+            rotated([(2, w_k)], k_t[:, 2:3, :], nc.gpsimd)
+            rotated([(3, w_k)], k_t[:, 3:4, :], nc.vector)
             v_tile(2)
             v_tile(3)

@@ -39,15 +39,22 @@ def tile_causalselfattention_pa_kernel(tc, x, cos, sin, w_words, w_scales, out_q
 
         xs = [keep.tile([P, NE], BF16, name="xs%d" % m, align_bytes=64) for m in range(MT)]
         xg = [[keep.tile([P, NE // 2], BF16, name="xg%d_%d" % (m, b), align_bytes=64) for b in range(2)] for m in range(MT)]
-        xc = [[keep.tile([P, NE // 8], U32, name="xc%d_%d" % (m, b), align_bytes=64) for b in range(2)] for m in range(MT)]
-        xsc = [[keep.tile([P, NE // 8], U8, name="xsc%d_%d" % (m, b), align_bytes=64) for b in range(2)] for m in range(MT)]
-        wq0 = [keep.tile([P, 1024], U8, name="wq0g%d" % g, align_bytes=64) for g in range(PASSES)]
-        wq = [None] + [keep.tile([P, PASSES, 1024], U8, name="wq%d" % grp, align_bytes=64) for grp in range(1, GROUPS)]
-        wk = keep.tile([P, PASSES, 1024], U8, name="wk", align_bytes=64)
-        wv = keep.tile([P, PASSES, 1024], U8, name="wv", align_bytes=64)
-        sc_all = keep.tile([P, GROUPS, PASSES, GCOLS], U8, name="sc_all", align_bytes=64)
-        sck = keep.tile([P, PASSES, 512], U8, name="sck", align_bytes=64)
-        scv = keep.tile([P, PASSES, 512], U8, name="scv", align_bytes=64)
+        xc_t = [[keep.tile([P, 16 + NE // 8], U32, name="xc%d_%d" % (m, b), align_bytes=256) for b in range(2)] for m in range(MT)]
+        xsc_t = [[keep.tile([P, 192 + NE // 8], U8, name="xsc%d_%d" % (m, b), align_bytes=256) for b in range(2)] for m in range(MT)]
+        xc = [[xc_t[m][b][:, 16:] for b in range(2)] for m in range(MT)]
+        xsc = [[xsc_t[m][b][:, 192:] for b in range(2)] for m in range(MT)]
+        wq0 = [keep.tile([P, 1024], U8, name="wq0g%d" % g, align_bytes=256) for g in range(PASSES)]
+        wq = [None] + [keep.tile([P, PASSES, 1024], U8, name="wq%d" % grp, align_bytes=256) for grp in range(1, GROUPS)]
+        wk = keep.tile([P, PASSES, 1024], U8, name="wk", align_bytes=256)
+        wv = keep.tile([P, PASSES, 1024], U8, name="wv", align_bytes=256)
+        sc_all_t = keep.tile([P, 128 + GROUPS * PASSES * GCOLS], U8, name="sc_all", align_bytes=256)
+        sc_all = sc_all_t[:, 128:].rearrange("p (grp g n) -> p grp g n", grp=GROUPS, g=PASSES)
+        scq0_t = keep.tile([P, 128 + PASSES * 512], U8, name="scq0", align_bytes=256)
+        scq0 = scq0_t[:, 128:].rearrange("p (g n) -> p g n", g=PASSES)
+        sck_t = keep.tile([P, 128 + PASSES * 512], U8, name="sck", align_bytes=256)
+        sck = sck_t[:, 128:].rearrange("p (g n) -> p g n", g=PASSES)
+        scv_t = keep.tile([P, 128 + PASSES * 512], U8, name="scv", align_bytes=256)
+        scv = scv_t[:, 128:].rearrange("p (g n) -> p g n", g=PASSES)
         craw = keep.tile([P, MT, HH], BF16, name="craw")
         sraw = keep.tile([P, MT, HH], BF16, name="sraw")
         tab = keep.tile([P, MT, 2, HS], F32, name="tab")
@@ -63,7 +70,7 @@ def tile_causalselfattention_pa_kernel(tc, x, cos, sin, w_words, w_scales, out_q
         def passes_of(codes, scales):
             return [(codes[:, g, :], scales[:, g, 0:512]) for g in range(PASSES)]
 
-        w_q = [[(wq0[g][:], sc_all[:, 0, g, 0:512]) for g in range(PASSES)]]
+        w_q = [[(wq0[g][:], scq0[:, g, :]) for g in range(PASSES)]]
         w_q += [passes_of(wq[grp], sc_all[:, grp]) for grp in range(1, GROUPS)]
         w_k = passes_of(wk, sck)
         w_v = passes_of(wv, scv)
@@ -72,6 +79,7 @@ def tile_causalselfattention_pa_kernel(tc, x, cos, sin, w_words, w_scales, out_q
             nc.vector.memset(zeros[:], 0.0)
             nc.vector.memset(warm_in[:], 0.0)
             nc.scalar.copy(out=warm_out[:], in_=warm_in[:])
+            nc.vector.memset(scq0.rearrange("p g n -> p (g n)").bitcast(I32), 0)
             for grp in range(GROUPS):
                 nc.vector.memset(sc_all[:, grp].rearrange("p g n -> p (g n)").bitcast(I32), 0)
 
@@ -102,7 +110,11 @@ def tile_causalselfattention_pa_kernel(tc, x, cos, sin, w_words, w_scales, out_q
 
             load_x(0)
             load_x(1)
-            load_scales(0)
+            for qd in range(4):
+                nc.sync.dma_start(
+                    out=scq0[32 * qd : 32 * qd + 4, :, :].bitcast(I32),
+                    in_=w_scales[:, 4 * qd : 4 * qd + 4, 0:512].rearrange("g r n -> r g n").bitcast(I32),
+                )
             for g in range(PASSES):
                 nc.sync.dma_start(out=wq0[g][:].bitcast(I32), in_=w_words[g, :, 0:1024].bitcast(I32))
             nc.sync.dma_start(out=craw[:], in_=cos.rearrange("(p m) i -> p m i", m=MT))
@@ -112,6 +124,7 @@ def tile_causalselfattention_pa_kernel(tc, x, cos, sin, w_words, w_scales, out_q
             for grp in range(1, GROUPS):
                 load_scales(grp)
                 load_wq(grp)
+            load_scales(0)
 
             idle_bank = psum.tile([P, 512], F32, name="bank", tag="bank")
 
@@ -140,7 +153,7 @@ def tile_causalselfattention_pa_kernel(tc, x, cos, sin, w_words, w_scales, out_q
 
             def quantize_x(m):
                 for b in range(2):
-                    nc.vector.quantize_mx(out=xc[m][b][:].bitcast(E5M2X4), scales=xsc[m][b][:], in_=xg[m][b][:])
+                    nc.vector.quantize_mx(out=xc[m][b].bitcast(E5M2X4), scales=xsc[m][b], in_=xg[m][b][:])
 
             def project(m, w_tile):
                 acc = psum.tile([P, 512], F32, name="bank", tag="bank")
@@ -216,16 +229,16 @@ def tile_causalselfattention_pa_kernel(tc, x, cos, sin, w_words, w_scales, out_q
             q_two_tokens(0, 1)
             load_wkv(wk, 1024)
             q_two_tokens(2, 1)
-            nat = sc_all[:].bitcast(I32)
+            nat = sc_all.bitcast(I32)
             nc.vector.tensor_copy(
-                out=scv[:].bitcast(I32).rearrange("p g (grp c) -> p g grp c", grp=GROUPS),
+                out=scv.bitcast(I32).rearrange("p g (grp c) -> p g grp c", grp=GROUPS),
                 in_=nat[:, :, :, 160:192].rearrange("p grp g c -> p g grp c"),
             )
             q_two_groups(0, 2)
             q_two_groups(1, 2)
             v_tile(0)
             nc.vector.tensor_copy(
-                out=sck[:].bitcast(I32).rearrange("p g (grp c) -> p g grp c", grp=GROUPS),
+                out=sck.bitcast(I32).rearrange("p g (grp c) -> p g grp c", grp=GROUPS),
                 in_=nat[:, :, :, 128:160].rearrange("p grp g c -> p g grp c"),
             )
             q_two_groups(2, 2)

@@ -37,7 +37,7 @@ def tile_causalselfattention_pa_kernel(tc, x, cos, sin, w_words, w_scales, out_q
         ident = keep.tile([P, P], F32, name="ident")
         make_identity(nc, ident[:])
 
-        xs = [keep.tile([P, NE], BF16, name="xs%d" % m, align_bytes=64) for m in range(MT)]
+        xs = [[keep.tile([P, NE // 2], BF16, name="xs%d_%d" % (m, b), align_bytes=64) for b in range(2)] for m in range(MT)]
         xg = [[keep.tile([P, NE // 2], BF16, name="xg%d_%d" % (m, b), align_bytes=64) for b in range(2)] for m in range(MT)]
         xc_t = [[keep.tile([P, 16 + NE // 8], U32, name="xc%d_%d" % (m, b), align_bytes=256) for b in range(2)] for m in range(MT)]
         xsc_t = [[keep.tile([P, 192 + NE // 8], U8, name="xsc%d_%d" % (m, b), align_bytes=256) for b in range(2)] for m in range(MT)]
@@ -84,7 +84,8 @@ def tile_causalselfattention_pa_kernel(tc, x, cos, sin, w_words, w_scales, out_q
                 nc.vector.memset(sc_all[:, grp].rearrange("p g n -> p (g n)").bitcast(I32), 0)
 
             def load_x(m):
-                nc.sync.dma_start(out=xs[m][:], in_=x_t[m])
+                for b in range(2):
+                    nc.sync.dma_start(out=xs[m][b][:], in_=x_t[m][:, (NE // 2) * b : (NE // 2) * (b + 1)])
 
             def load_scales(grp):
                 for qd in range(4):
@@ -108,8 +109,8 @@ def tile_causalselfattention_pa_kernel(tc, x, cos, sin, w_words, w_scales, out_q
                         in_=w_words[g].rearrange("p (grp c) -> p grp c", grp=GROUPS)[:, :, first_byte : first_byte + 256].bitcast(I32),
                     )
 
-            load_x(0)
-            load_x(1)
+            for m in range(MT):
+                load_x(m)
             for qd in range(4):
                 nc.sync.dma_start(
                     out=scq0[32 * qd : 32 * qd + 4, :, :].bitcast(I32),
@@ -119,8 +120,6 @@ def tile_causalselfattention_pa_kernel(tc, x, cos, sin, w_words, w_scales, out_q
                 nc.sync.dma_start(out=wq0[g][:].bitcast(I32), in_=w_words[g, :, 0:1024].bitcast(I32))
             nc.sync.dma_start(out=craw[:], in_=cos.rearrange("(p m) i -> p m i", m=MT))
             nc.sync.dma_start(out=sraw[:], in_=sin.rearrange("(p m) i -> p m i", m=MT))
-            load_x(2)
-            load_x(3)
             for grp in range(1, GROUPS):
                 load_scales(grp)
                 load_wq(grp)
@@ -132,27 +131,20 @@ def tile_causalselfattention_pa_kernel(tc, x, cos, sin, w_words, w_scales, out_q
                 for i in range(n):
                     nc.tensor.matmul(out=idle_bank[:], lhsT=zeros[:, 0:P], rhs=zeros[:], start=True, stop=True)
 
-            def transpose_x(m, both_engines):
-                words = xs[m][:].bitcast(F32)
+            def transpose_x(m):
                 for b in range(2):
+                    words = xs[m][b][:].bitcast(F32)
                     grouped = xg[m][b][:].bitcast(F32).rearrange("p (gl r u) -> p gl r u", gl=2, u=2)
                     xt = psum.tile([P, 512], F32, name="bank", tag="bank")
                     for gl in range(2):
-                        g = 2 * b + gl
                         for u in range(2):
                             nc.tensor.transpose(
                                 out=xt[:, P * (2 * gl + u) : P * (2 * gl + u + 1)],
-                                in_=words[:, 256 * g + u : 256 * (g + 1) : 2],
+                                in_=words[:, 256 * gl + u : 256 * (gl + 1) : 2],
                                 identity=ident[:],
                             )
                     src = xt[:].rearrange("p (gl u r) -> p gl r u", gl=2, u=2)
-                    if both_engines and b == 0:
-                        nc.vector.tensor_copy(out=grouped, in_=src)
-                    else:
-                        nc.scalar.copy(out=grouped, in_=src)
-
-            def quantize_x(m):
-                for b in range(2):
+                    nc.scalar.copy(out=grouped, in_=src)
                     nc.vector.quantize_mx(out=xc[m][b].bitcast(E5M2X4), scales=xsc[m][b], in_=xg[m][b][:])
 
             def project(m, w_tile):
@@ -207,12 +199,11 @@ def tile_causalselfattention_pa_kernel(tc, x, cos, sin, w_words, w_scales, out_q
                 nc.scalar.copy(out=res[:], in_=acc[:])
                 nc.scalar.dma_start(out=v_t[:, m, :], in_=res[:])
 
-            keep_warm(4)
-            transpose_x(0, True)
-            quantize_x(0)
-            keep_warm(1)
-            transpose_x(1, True)
-            quantize_x(1)
+            keep_warm(3)
+            for m in range(MT):
+                transpose_x(m)
+                if m < MT - 1:
+                    keep_warm(1)
             nc.vector.tensor_copy(
                 out=tab[:, :, 0, :].rearrange("p m (s i) -> p m s i", s=2),
                 in_=craw[:].unsqueeze(2).to_broadcast([P, MT, 2, HH]),
@@ -221,10 +212,6 @@ def tile_causalselfattention_pa_kernel(tc, x, cos, sin, w_words, w_scales, out_q
             nc.scalar.mul(out=tab[:, :, 1, HH:HS], in_=sraw[:], mul=-1.0)
             q_two_tokens(0, 0)
             load_wkv(wv, 1280)
-            transpose_x(2, False)
-            quantize_x(2)
-            transpose_x(3, False)
-            quantize_x(3)
             q_two_tokens(2, 0)
             q_two_tokens(0, 1)
             load_wkv(wk, 1024)

@@ -109,8 +109,17 @@ def tile_causalselfattention_pa_kernel(tc, x, cos, sin, w_words, w_scales, out_q
                         in_=w_words[g].rearrange("p (grp c) -> p grp c", grp=GROUPS)[:, :, first_byte : first_byte + 256].bitcast(I32),
                     )
 
+            def gather_scales(dst, first_column):
+                for g in range(PASSES):
+                    nc.sync.dma_start(
+                        out=dst[:, g, :].bitcast(I32).rearrange("p (grp c) -> p grp c", grp=GROUPS),
+                        in_=sc_all[:, :, g, first_column : first_column + HS].bitcast(I32),
+                    )
+
             for m in range(MT):
                 load_x(m)
+            nc.sync.dma_start(out=craw[:], in_=cos.rearrange("(p m) i -> p m i", m=MT))
+            nc.sync.dma_start(out=sraw[:], in_=sin.rearrange("(p m) i -> p m i", m=MT))
             for qd in range(4):
                 nc.sync.dma_start(
                     out=scq0[32 * qd : 32 * qd + 4, :, :].bitcast(I32),
@@ -118,8 +127,6 @@ def tile_causalselfattention_pa_kernel(tc, x, cos, sin, w_words, w_scales, out_q
                 )
             for g in range(PASSES):
                 nc.sync.dma_start(out=wq0[g][:].bitcast(I32), in_=w_words[g, :, 0:1024].bitcast(I32))
-            nc.sync.dma_start(out=craw[:], in_=cos.rearrange("(p m) i -> p m i", m=MT))
-            nc.sync.dma_start(out=sraw[:], in_=sin.rearrange("(p m) i -> p m i", m=MT))
             for grp in range(1, GROUPS):
                 load_scales(grp)
                 load_wq(grp)
@@ -200,38 +207,36 @@ def tile_causalselfattention_pa_kernel(tc, x, cos, sin, w_words, w_scales, out_q
                 nc.scalar.dma_start(out=v_t[:, m, :], in_=res[:])
 
             keep_warm(3)
+            def rotary_tables():
+                nc.vector.tensor_copy(
+                    out=tab[:, :, 0, :].rearrange("p m (s i) -> p m s i", s=2),
+                    in_=craw[:].unsqueeze(2).to_broadcast([P, MT, 2, HH]),
+                )
+                nc.vector.tensor_copy(out=tab[:, :, 1, 0:HH], in_=sraw[:])
+                nc.vector.tensor_scalar_mul(out=tab[:, :, 1, HH:HS], in0=sraw[:], scalar1=-1.0)
+
             for m in range(MT):
+                if m == MT - 1:
+                    rotary_tables()
                 transpose_x(m)
                 if m < MT - 1:
                     keep_warm(1)
-            nc.vector.tensor_copy(
-                out=tab[:, :, 0, :].rearrange("p m (s i) -> p m s i", s=2),
-                in_=craw[:].unsqueeze(2).to_broadcast([P, MT, 2, HH]),
-            )
-            nc.scalar.copy(out=tab[:, :, 1, 0:HH], in_=sraw[:])
-            nc.scalar.mul(out=tab[:, :, 1, HH:HS], in_=sraw[:], mul=-1.0)
             q_two_tokens(0, 0)
             load_wkv(wv, 1280)
+            gather_scales(scv, 640)
             q_two_tokens(2, 0)
             q_two_tokens(0, 1)
             load_wkv(wk, 1024)
+            gather_scales(sck, 512)
             q_two_tokens(2, 1)
-            nat = sc_all.bitcast(I32)
-            nc.vector.tensor_copy(
-                out=scv.bitcast(I32).rearrange("p g (grp c) -> p g grp c", grp=GROUPS),
-                in_=nat[:, :, :, 160:192].rearrange("p grp g c -> p g grp c"),
-            )
             q_two_groups(0, 2)
             q_two_groups(1, 2)
             v_tile(0)
-            nc.vector.tensor_copy(
-                out=sck.bitcast(I32).rearrange("p g (grp c) -> p g grp c", grp=GROUPS),
-                in_=nat[:, :, :, 128:160].rearrange("p grp g c -> p g grp c"),
-            )
             q_two_groups(2, 2)
             q_two_groups(3, 2)
             v_tile(1)
-            rotated([(0, w_k), (1, w_k)], k_t[:, 0:2, :], nc.gpsimd)
+            rotated([(0, w_k)], k_t[:, 0:1, :], nc.gpsimd)
+            rotated([(1, w_k)], k_t[:, 1:2, :], nc.gpsimd)
             rotated([(2, w_k)], k_t[:, 2:3, :], nc.gpsimd)
             rotated([(3, w_k)], k_t[:, 3:4, :], nc.vector)
             v_tile(2)

@@ -29,21 +29,23 @@ def tile_causalselfattention_pa_kernel(tc, x, cos, sin, w_words, w_scales, out_q
     nc = tc.nc
     with ExitStack() as ctx:
         keep = ctx.enter_context(tc.tile_pool(name="keep", bufs=1))
-        prod_pool = ctx.enter_context(tc.tile_pool(name="prod", bufs=4))
-        res_pool = ctx.enter_context(tc.tile_pool(name="res", bufs=4))
+        prod_pool = ctx.enter_context(tc.tile_pool(name="prod", bufs=8))
+        res_pool = ctx.enter_context(tc.tile_pool(name="res", bufs=8))
         vres_pool = ctx.enter_context(tc.tile_pool(name="vres", bufs=4))
         psum = ctx.enter_context(tc.psum_pool(name="psum", bufs=8))
 
         ident = keep.tile([P, P], F32, name="ident")
         make_identity(nc, ident[:])
 
-        xs = [[keep.tile([P, NE // 2], BF16, name="xs%d_%d" % (m, b), align_bytes=64) for b in range(2)] for m in range(MT)]
+        xs0 = [keep.tile([P, NE // 2], BF16, name="xs0_%d" % b, align_bytes=64) for b in range(2)]
+        xs_rest = [keep.tile([P, NE], BF16, name="xs%d" % m, align_bytes=64) for m in range(1, MT)]
+        xs = [[t[:] for t in xs0]] + [[t[:, (NE // 2) * b : (NE // 2) * (b + 1)] for b in range(2)] for t in xs_rest]
         xg = [[keep.tile([P, NE // 2], BF16, name="xg%d_%d" % (m, b), align_bytes=64) for b in range(2)] for m in range(MT)]
         xc_t = [[keep.tile([P, 16 + NE // 8], U32, name="xc%d_%d" % (m, b), align_bytes=256) for b in range(2)] for m in range(MT)]
         xsc_t = [[keep.tile([P, 192 + NE // 8], U8, name="xsc%d_%d" % (m, b), align_bytes=256) for b in range(2)] for m in range(MT)]
         xc = [[xc_t[m][b][:, 16:] for b in range(2)] for m in range(MT)]
         xsc = [[xsc_t[m][b][:, 192:] for b in range(2)] for m in range(MT)]
-        wq0 = [keep.tile([P, 1024], U8, name="wq0g%d" % g, align_bytes=256) for g in range(PASSES)]
+        wq0 = [keep.tile([P, 2, 1024], U8, name="wq0b%d" % b, align_bytes=256) for b in range(2)]
         wq = [None] + [keep.tile([P, PASSES, 1024], U8, name="wq%d" % grp, align_bytes=256) for grp in range(1, GROUPS)]
         wk = keep.tile([P, PASSES, 1024], U8, name="wk", align_bytes=256)
         wv = keep.tile([P, PASSES, 1024], U8, name="wv", align_bytes=256)
@@ -70,7 +72,7 @@ def tile_causalselfattention_pa_kernel(tc, x, cos, sin, w_words, w_scales, out_q
         def passes_of(codes, scales):
             return [(codes[:, g, :], scales[:, g, 0:512]) for g in range(PASSES)]
 
-        w_q = [[(wq0[g][:], scq0[:, g, :]) for g in range(PASSES)]]
+        w_q = [[(wq0[g // 2][:, g % 2, :], scq0[:, g, :]) for g in range(PASSES)]]
         w_q += [passes_of(wq[grp], sc_all[:, grp]) for grp in range(1, GROUPS)]
         w_k = passes_of(wk, sck)
         w_v = passes_of(wv, scv)
@@ -82,10 +84,6 @@ def tile_causalselfattention_pa_kernel(tc, x, cos, sin, w_words, w_scales, out_q
             nc.vector.memset(scq0.rearrange("p g n -> p (g n)").bitcast(I32), 0)
             for grp in range(GROUPS):
                 nc.vector.memset(sc_all[:, grp].rearrange("p g n -> p (g n)").bitcast(I32), 0)
-
-            def load_x(m):
-                for b in range(2):
-                    nc.sync.dma_start(out=xs[m][b][:], in_=x_t[m][:, (NE // 2) * b : (NE // 2) * (b + 1)])
 
             def load_scales(grp):
                 for qd in range(4):
@@ -116,17 +114,22 @@ def tile_causalselfattention_pa_kernel(tc, x, cos, sin, w_words, w_scales, out_q
                         in_=sc_all[:, :, g, first_column : first_column + HS].bitcast(I32),
                     )
 
-            for m in range(MT):
-                load_x(m)
+            for b in range(2):
+                nc.sync.dma_start(out=xs[0][b], in_=x_t[0][:, (NE // 2) * b : (NE // 2) * (b + 1)])
             nc.sync.dma_start(out=craw[:], in_=cos.rearrange("(p m) i -> p m i", m=MT))
             nc.sync.dma_start(out=sraw[:], in_=sin.rearrange("(p m) i -> p m i", m=MT))
+            for m in range(1, MT):
+                nc.sync.dma_start(out=xs_rest[m - 1][:], in_=x_t[m])
             for qd in range(4):
                 nc.sync.dma_start(
                     out=scq0[32 * qd : 32 * qd + 4, :, :].bitcast(I32),
                     in_=w_scales[:, 4 * qd : 4 * qd + 4, 0:512].rearrange("g r n -> r g n").bitcast(I32),
                 )
-            for g in range(PASSES):
-                nc.sync.dma_start(out=wq0[g][:].bitcast(I32), in_=w_words[g, :, 0:1024].bitcast(I32))
+            for b in range(2):
+                nc.sync.dma_start(
+                    out=wq0[b][:].bitcast(I32),
+                    in_=w_words[2 * b : 2 * b + 2, :, 0:1024].rearrange("g p b -> p g b").bitcast(I32),
+                )
             for grp in range(1, GROUPS):
                 load_scales(grp)
                 load_wq(grp)
@@ -140,7 +143,7 @@ def tile_causalselfattention_pa_kernel(tc, x, cos, sin, w_words, w_scales, out_q
 
             def transpose_x(m):
                 for b in range(2):
-                    words = xs[m][b][:].bitcast(F32)
+                    words = xs[m][b].bitcast(F32)
                     grouped = xg[m][b][:].bitcast(F32).rearrange("p (gl r u) -> p gl r u", gl=2, u=2)
                     xt = psum.tile([P, 512], F32, name="bank", tag="bank")
                     for gl in range(2):
@@ -171,7 +174,7 @@ def tile_causalselfattention_pa_kernel(tc, x, cos, sin, w_words, w_scales, out_q
 
             def rotated(tiles, dst, sum_engine):
                 n = len(tiles)
-                prod = prod_pool.tile([P, 2, n * 512], F32, name="prod%d" % n)
+                prod = prod_pool.tile([P, 2, n * 512], F32, name="prod%d" % n, bufs=8 if n == 2 else 4)
                 for tl in range(n):
                     m, w_tile = tiles[tl]
                     acc = project(m, w_tile)
@@ -181,7 +184,7 @@ def tile_causalselfattention_pa_kernel(tc, x, cos, sin, w_words, w_scales, out_q
                         in1=tab[:, m].unsqueeze(2).to_broadcast([P, 2, 4, HS]),
                         op=MULT,
                     )
-                res = res_pool.tile([P, n * 512], F32, name="res%d" % n)
+                res = res_pool.tile([P, n * 512], F32, name="res%d" % n, bufs=8 if n == 2 else 4)
                 sum_engine.tensor_tensor(
                     out=res[:].rearrange("p (h s i) -> p h s i", s=2, i=HH),
                     in0=prod[:, 0].rearrange("p (h s i) -> p h s i", s=2, i=HH),

@@ -172,7 +172,7 @@ def tile_causalselfattention_pa_kernel(tc, x, cos, sin, w_words, w_scales, out_q
                     )
                 return acc
 
-            def rotated(tiles, dst, sum_engine):
+            def products(tiles):
                 n = len(tiles)
                 prod = prod_pool.tile([P, 2, n * 512], F32, name="prod%d" % n, bufs=8 if n == 2 else 4)
                 for tl in range(n):
@@ -184,6 +184,9 @@ def tile_causalselfattention_pa_kernel(tc, x, cos, sin, w_words, w_scales, out_q
                         in1=tab[:, m].unsqueeze(2).to_broadcast([P, 2, 4, HS]),
                         op=MULT,
                     )
+                return prod
+
+            def sum_and_store(n, prod, dst, sum_engine):
                 res = res_pool.tile([P, n * 512], F32, name="res%d" % n, bufs=8 if n == 2 else 4)
                 sum_engine.tensor_tensor(
                     out=res[:].rearrange("p (h s i) -> p h s i", s=2, i=HH),
@@ -192,6 +195,9 @@ def tile_causalselfattention_pa_kernel(tc, x, cos, sin, w_words, w_scales, out_q
                     op=ADD,
                 )
                 nc.sync.dma_start(out=dst, in_=res[:].rearrange("p (tl c) -> p tl c", tl=n))
+
+            def rotated(tiles, dst, sum_engine):
+                sum_and_store(len(tiles), products(tiles), dst, sum_engine)
 
             def q_two_tokens(m0, grp):
                 rotated([(m0 + tl, w_q[grp]) for tl in range(2)], q_t[:, m0 : m0 + 2, 512 * grp : 512 * (grp + 1)], nc.gpsimd)
@@ -240,7 +246,8 @@ def tile_causalselfattention_pa_kernel(tc, x, cos, sin, w_words, w_scales, out_q
             v_tile(1)
             rotated([(0, w_k)], k_t[:, 0:1, :], nc.gpsimd)
             rotated([(1, w_k)], k_t[:, 1:2, :], nc.gpsimd)
-            rotated([(2, w_k)], k_t[:, 2:3, :], nc.gpsimd)
-            rotated([(3, w_k)], k_t[:, 3:4, :], nc.vector)
+            last_keys = [products([(m, w_k)]) for m in (2, 3)]
+            for m in (2, 3):
+                sum_and_store(1, last_keys[m - 2], k_t[:, m : m + 1, :], nc.vector)
             v_tile(2)
             v_tile(3)

from contextlib import ExitStack

import concourse.mybir as mybir
from concourse.masks import make_identity

F32 = mybir.dt.float32
BF16 = mybir.dt.bfloat16
I32 = mybir.dt.int32
U32 = mybir.dt.uint32
U8 = mybir.dt.uint8
E5M2X4 = mybir.dt.float8_e5m2_x4
E2M1X4 = mybir.dt.float4_e2m1fn_x4
ADD = mybir.AluOpType.add
MULT = mybir.AluOpType.mult

T, NE, NOUT = 512, 2048, 3072
FLOPS = 2 * T * NE * NOUT

P = 128
PASSES = NE // 512
MT = T // P
GROUPS = 4
GCOLS = 768
HS = 128
HH = 64


def tile_causalselfattention_pa_kernel(tc, x, cos, sin, w_words, w_scales, out_q, out_k, out_v):
    nc = tc.nc
    with ExitStack() as ctx:
        keep = ctx.enter_context(tc.tile_pool(name="keep", bufs=1))
        prod_pool = ctx.enter_context(tc.tile_pool(name="prod", bufs=8))
        res_pool = ctx.enter_context(tc.tile_pool(name="res", bufs=8))
        vres_pool = ctx.enter_context(tc.tile_pool(name="vres", bufs=4))
        psum = ctx.enter_context(tc.psum_pool(name="psum", bufs=8))

        ident = keep.tile([P, P], F32, name="ident")
        make_identity(nc, ident[:])

        xs0 = [keep.tile([P, NE // 2], BF16, name="xs0_%d" % b, align_bytes=64) for b in range(2)]
        xs_rest = [keep.tile([P, NE], BF16, name="xs%d" % m, align_bytes=64) for m in range(1, MT)]
        xs = [[t[:] for t in xs0]] + [[t[:, (NE // 2) * b : (NE // 2) * (b + 1)] for b in range(2)] for t in xs_rest]
        xg = [[keep.tile([P, NE // 2], BF16, name="xg%d_%d" % (m, b), align_bytes=64) for b in range(2)] for m in range(MT)]
        xc_t = [[keep.tile([P, 16 + NE // 8], U32, name="xc%d_%d" % (m, b), align_bytes=256) for b in range(2)] for m in range(MT)]
        xsc_t = [[keep.tile([P, 192 + NE // 8], U8, name="xsc%d_%d" % (m, b), align_bytes=256) for b in range(2)] for m in range(MT)]
        xc = [[xc_t[m][b][:, 16:] for b in range(2)] for m in range(MT)]
        xsc = [[xsc_t[m][b][:, 192:] for b in range(2)] for m in range(MT)]
        wq0 = [keep.tile([P, 2, 1024], U8, name="wq0b%d" % b, align_bytes=256) for b in range(2)]
        wq = [None] + [keep.tile([P, PASSES, 1024], U8, name="wq%d" % grp, align_bytes=256) for grp in range(1, GROUPS)]
        wk = keep.tile([P, PASSES, 1024], U8, name="wk", align_bytes=256)
        wv = keep.tile([P, PASSES, 1024], U8, name="wv", align_bytes=256)
        sc_all_t = keep.tile([P, 128 + GROUPS * PASSES * GCOLS], U8, name="sc_all", align_bytes=256)
        sc_all = sc_all_t[:, 128:].rearrange("p (grp g n) -> p grp g n", grp=GROUPS, g=PASSES)
        scq0_t = keep.tile([P, 128 + PASSES * 512], U8, name="scq0", align_bytes=256)
        scq0 = scq0_t[:, 128:].rearrange("p (g n) -> p g n", g=PASSES)
        sck_t = keep.tile([P, 128 + PASSES * 512], U8, name="sck", align_bytes=256)
        sck = sck_t[:, 128:].rearrange("p (g n) -> p g n", g=PASSES)
        scv_t = keep.tile([P, 128 + PASSES * 512], U8, name="scv", align_bytes=256)
        scv = scv_t[:, 128:].rearrange("p (g n) -> p g n", g=PASSES)
        craw = keep.tile([P, MT, HH], BF16, name="craw")
        sraw = keep.tile([P, MT, HH], BF16, name="sraw")
        tab = keep.tile([P, MT, 2, HS], F32, name="tab")
        warm_in = keep.tile([P, 8], F32, name="warm_in")
        warm_out = keep.tile([P, 8], F32, name="warm_out")
        zeros = keep.tile([P, 512], BF16, name="zeros")

        x_t = x[0].rearrange("(p m) k -> m p k", m=MT)
        q_t = out_q[0].rearrange("(p m) h e -> p m (h e)", m=MT)
        k_t = out_k[0].rearrange("(p m) h e -> p m (h e)", m=MT)
        v_t = out_v[0].rearrange("(p m) h e -> p m (h e)", m=MT)

        def passes_of(codes, scales):
            return [(codes[:, g, :], scales[:, g, 0:512]) for g in range(PASSES)]

        w_q = [[(wq0[g // 2][:, g % 2, :], scq0[:, g, :]) for g in range(PASSES)]]
        w_q += [passes_of(wq[grp], sc_all[:, grp]) for grp in range(1, GROUPS)]
        w_k = passes_of(wk, sck)
        w_v = passes_of(wv, scv)

        with tc.manual_schedule():
            nc.vector.memset(zeros[:], 0.0)
            nc.vector.memset(warm_in[:], 0.0)
            nc.scalar.copy(out=warm_out[:], in_=warm_in[:])
            nc.vector.memset(scq0.rearrange("p g n -> p (g n)").bitcast(I32), 0)
            for grp in range(GROUPS):
                nc.vector.memset(sc_all[:, grp].rearrange("p g n -> p (g n)").bitcast(I32), 0)

            def load_scales(grp):
                for qd in range(4):
                    nc.sync.dma_start(
                        out=sc_all[32 * qd : 32 * qd + 4, grp, :, :].bitcast(I32),
                        in_=w_scales[:, 4 * qd : 4 * qd + 4, GCOLS * grp : GCOLS * (grp + 1)]
                        .rearrange("g r n -> r g n")
                        .bitcast(I32),
                    )

            def load_wq(grp):
                nc.sync.dma_start(
                    out=wq[grp][:].bitcast(I32),
                    in_=w_words[:, :, 2 * GCOLS * grp : 2 * GCOLS * grp + 1024].rearrange("g p b -> p g b").bitcast(I32),
                )

            def load_wkv(dst, first_byte):
                for g in range(PASSES):
                    nc.sync.dma_start(
                        out=dst[:, g, :].bitcast(I32).rearrange("p (grp c) -> p grp c", grp=GROUPS),
                        in_=w_words[g].rearrange("p (grp c) -> p grp c", grp=GROUPS)[:, :, first_byte : first_byte + 256].bitcast(I32),
                    )

            def gather_scales(dst, first_column):
                for g in range(PASSES):
                    nc.sync.dma_start(
                        out=dst[:, g, :].bitcast(I32).rearrange("p (grp c) -> p grp c", grp=GROUPS),
                        in_=sc_all[:, :, g, first_column : first_column + HS].bitcast(I32),
                    )

            for b in range(2):
                nc.sync.dma_start(out=xs[0][b], in_=x_t[0][:, (NE // 2) * b : (NE // 2) * (b + 1)])
            nc.sync.dma_start(out=craw[:], in_=cos.rearrange("(p m) i -> p m i", m=MT))
            nc.sync.dma_start(out=sraw[:], in_=sin.rearrange("(p m) i -> p m i", m=MT))
            for m in range(1, MT):
                nc.sync.dma_start(out=xs_rest[m - 1][:], in_=x_t[m])
            for qd in range(4):
                nc.sync.dma_start(
                    out=scq0[32 * qd : 32 * qd + 4, :, :].bitcast(I32),
                    in_=w_scales[:, 4 * qd : 4 * qd + 4, 0:512].rearrange("g r n -> r g n").bitcast(I32),
                )
            for b in range(2):
                nc.sync.dma_start(
                    out=wq0[b][:].bitcast(I32),
                    in_=w_words[2 * b : 2 * b + 2, :, 0:1024].rearrange("g p b -> p g b").bitcast(I32),
                )
            for grp in range(1, GROUPS):
                load_scales(grp)
                load_wq(grp)
            load_scales(0)

            idle_bank = psum.tile([P, 512], F32, name="bank", tag="bank")

            def keep_warm(n):
                for i in range(n):
                    nc.tensor.matmul(out=idle_bank[:], lhsT=zeros[:, 0:P], rhs=zeros[:], start=True, stop=True)

            def transpose_x(m):
                for b in range(2):
                    words = xs[m][b].bitcast(F32)
                    grouped = xg[m][b][:].bitcast(F32).rearrange("p (gl r u) -> p gl r u", gl=2, u=2)
                    xt = psum.tile([P, 512], F32, name="bank", tag="bank")
                    for gl in range(2):
                        for u in range(2):
                            nc.tensor.transpose(
                                out=xt[:, P * (2 * gl + u) : P * (2 * gl + u + 1)],
                                in_=words[:, 256 * gl + u : 256 * (gl + 1) : 2],
                                identity=ident[:],
                            )
                    src = xt[:].rearrange("p (gl u r) -> p gl r u", gl=2, u=2)
                    nc.scalar.copy(out=grouped, in_=src)
                    nc.vector.quantize_mx(out=xc[m][b].bitcast(E5M2X4), scales=xsc[m][b], in_=xg[m][b][:])

            def project(m, w_tile):
                acc = psum.tile([P, 512], F32, name="bank", tag="bank")
                for g in range(PASSES):
                    codes, scales = w_tile[g]
                    nc.tensor.matmul_mx(
                        out=acc[:],
                        lhsT=xc[m][g // 2][:, P * (g % 2) : P * (g % 2 + 1)].bitcast(E5M2X4),
                        lhsT_scale=xsc[m][g // 2][:, P * (g % 2) : P * (g % 2 + 1)],
                        rhs=codes.bitcast(E2M1X4),
                        rhs_scale=scales,
                        start=(g == 0),
                        stop=(g == PASSES - 1),
                    )
                return acc

            def products(tiles):
                n = len(tiles)
                prod = prod_pool.tile([P, 2, n * 512], F32, name="prod%d" % n, bufs=8 if n == 2 else 4)
                for tl in range(n):
                    m, w_tile = tiles[tl]
                    acc = project(m, w_tile)
                    nc.vector.tensor_tensor(
                        out=prod[:, :, 512 * tl : 512 * (tl + 1)].rearrange("p w (h e) -> p w h e", h=4),
                        in0=acc[:].rearrange("p (h e) -> p h e", h=4).unsqueeze(1).to_broadcast([P, 2, 4, HS]),
                        in1=tab[:, m].unsqueeze(2).to_broadcast([P, 2, 4, HS]),
                        op=MULT,
                    )
                return prod

            def sum_and_store(n, prod, dst, sum_engine):
                res = res_pool.tile([P, n * 512], F32, name="res%d" % n, bufs=8 if n == 2 else 4)
                sum_engine.tensor_tensor(
                    out=res[:].rearrange("p (h s i) -> p h s i", s=2, i=HH),
                    in0=prod[:, 0].rearrange("p (h s i) -> p h s i", s=2, i=HH),
                    in1=prod[:, 1].rearrange("p (h s i) -> p h s i", s=2, i=HH)[:, :, ::-1, :],
                    op=ADD,
                )
                nc.sync.dma_start(out=dst, in_=res[:].rearrange("p (tl c) -> p tl c", tl=n))

            def rotated(tiles, dst, sum_engine):
                sum_and_store(len(tiles), products(tiles), dst, sum_engine)

            def q_two_tokens(m0, grp):
                rotated([(m0 + tl, w_q[grp]) for tl in range(2)], q_t[:, m0 : m0 + 2, 512 * grp : 512 * (grp + 1)], nc.gpsimd)

            def q_two_groups(m, grp0):
                rotated(
                    [(m, w_q[grp0 + tl]) for tl in range(2)],
                    q_t[:, m, 512 * grp0 : 512 * (grp0 + 2)].rearrange("p (tl c) -> p tl c", tl=2),
                    nc.gpsimd,
                )

            def v_tile(m):
                acc = project(m, w_v)
                res = vres_pool.tile([P, 512], F32, name="vres")
                nc.scalar.copy(out=res[:], in_=acc[:])
                nc.scalar.dma_start(out=v_t[:, m, :], in_=res[:])

            keep_warm(3)
            def rotary_tables():
                nc.vector.tensor_copy(
                    out=tab[:, :, 0, :].rearrange("p m (s i) -> p m s i", s=2),
                    in_=craw[:].unsqueeze(2).to_broadcast([P, MT, 2, HH]),
                )
                nc.vector.tensor_copy(out=tab[:, :, 1, 0:HH], in_=sraw[:])
                nc.vector.tensor_scalar_mul(out=tab[:, :, 1, HH:HS], in0=sraw[:], scalar1=-1.0)

            for m in range(MT):
                if m == MT - 1:
                    rotary_tables()
                transpose_x(m)
                if m < MT - 1:
                    keep_warm(1)
            q_two_tokens(0, 0)
            load_wkv(wv, 1280)
            gather_scales(scv, 640)
            q_two_tokens(2, 0)
            q_two_tokens(0, 1)
            load_wkv(wk, 1024)
            gather_scales(sck, 512)
            q_two_tokens(2, 1)
            q_two_groups(0, 2)
            q_two_groups(1, 2)
            v_tile(0)
            q_two_groups(2, 2)
            q_two_groups(3, 2)
            v_tile(1)
            rotated([(0, w_k)], k_t[:, 0:1, :], nc.gpsimd)
            rotated([(1, w_k)], k_t[:, 1:2, :], nc.gpsimd)
            last_keys = [products([(m, w_k)]) for m in (2, 3)]
            for m in (2, 3):
                sum_and_store(1, last_keys[m - 2], k_t[:, m : m + 1, :], nc.vector)
            v_tile(2)
            v_tile(3)
